import numpy as np
import ml_dtypes


def mxq(x, axis, fmt="e4m3"):
    dtype, down = {"e4m3": (ml_dtypes.float8_e4m3fn, 7), "e5m2": (ml_dtypes.float8_e5m2, 14)}[fmt]
    v = np.moveaxis(np.asarray(x, np.float32).astype(ml_dtypes.bfloat16).astype(np.float64), axis, -1)
    blocks = v.reshape(v.shape[:-1] + (-1, 32))
    amax = np.abs(blocks).max(-1, keepdims=True)
    byte = np.maximum(np.where(amax > 0, np.frexp(amax)[1] - 1 + 127, 0) - down, 1)
    scale = np.exp2(byte - 127.0)
    codes = (blocks / scale).astype(np.float32).astype(dtype).astype(np.float64)
    return np.moveaxis((codes * scale).reshape(v.shape), -1, axis)


WIDE = False


def mx_kscale(k):
    if not WIDE:
        return np.ones(k)
    levels = np.array([10, -10, 5, -5, 0])
    a = np.random.permutation(np.resize(levels, k // 512 * 4)).reshape(k // 512, 4)
    idx = np.arange(k)
    return np.exp2(a[idx // 512, idx % 128 // 32])


BF16 = ml_dtypes.bfloat16


def bf(x):
    return np.asarray(x, np.float32).astype(BF16)


def f64(x):
    return np.asarray(x).astype(np.float64)


E2M1 = np.array([0.0, 0.5, 1.0, 1.5, 2.0, 3.0, 4.0, 6.0, -0.0, -0.5, -1.0, -1.5, -2.0, -3.0, -4.0, -6.0])


def pack_weight(w, fmt):
    k, n = w.shape
    w = f64(bf(w)).reshape(k // 32, 32, n)
    amax = np.abs(w).max(1)
    if fmt == "e4m3":
        byte = np.frexp(amax)[1] - 1 + 127 - 7
    else:
        mant, ex = np.frexp(amax / 6.0)
        byte = np.where(mant > 0.5, ex, ex - 1) + 127
    byte = np.clip(np.where(amax > 0, byte, 1), 1, 254)
    scaled = (w * np.exp2(127.0 - byte)[:, None, :]).reshape(k, n).astype(np.float32)
    by_word = np.ascontiguousarray(scaled.reshape(k // 512, 128, 4, n).transpose(0, 1, 3, 2))
    if fmt == "e4m3":
        words = by_word.astype(ml_dtypes.float8_e4m3fn).view(np.uint8)
    else:
        c = by_word.astype(ml_dtypes.float4_e2m1fn).view(np.uint8) & 0xF
        words = c[..., 0::2] | (c[..., 1::2] << 4)
    return np.ascontiguousarray(words), np.ascontiguousarray(byte.astype(np.uint8).reshape(k // 512, 16, n))


def unpack_weight(words, scales, fmt):
    g, p, n, _ = words.shape
    if fmt == "e4m3":
        vals = np.ascontiguousarray(words).view(ml_dtypes.float8_e4m3fn).astype(np.float64)
    else:
        nib = np.empty((g, p, n, 4), np.uint8)
        nib[..., 0::2] = words & 0xF
        nib[..., 1::2] = words >> 4
        vals = E2M1[nib]
    vals = vals * np.repeat(np.exp2(scales.astype(np.float64) - 127.0), 8, axis=1)[..., None]
    return vals.transpose(0, 1, 3, 2).reshape(g * 512, n)

def pack4(w):
    words, scales = pack_weight(w, "e2m1")
    return words.reshape(words.shape[0], 128, -1), scales


def unpack4(words, scales):
    return unpack_weight(words.reshape(words.shape[0], 128, -1, 2), scales, "e2m1")


B, HH, WW, E, NH, D = 1, 512, 4, 1024, 8, 128
KD = NH * D


def setup_inputs():
    t = mx_kscale(KD)
    ret_w = bf(np.random.standard_normal((B, HH, WW, NH, D)) * 0.9)
    kv_h = bf(np.random.standard_normal((B, WW, NH, D, D)) * 0.8 * t.reshape(NH, 1, D))
    Wo_words, Wo_scales = pack4((np.random.standard_normal((E, KD)) * 0.3 / np.sqrt(KD) / t).T)
    bo = bf(np.random.standard_normal(E) * 0.2)
    return {"ret_w": ret_w,
            "kv_h": kv_h,
            "Wo_words": Wo_words,
            "Wo_scales": Wo_scales,
            "bo": bo}


def reference(ret_w, kv_h, Wo_words, Wo_scales, bo):
    o = f64(ret_w).reshape(B, HH, WW * NH, D).transpose(0, 2, 1, 3) @ f64(kv_h).reshape(B, WW * NH, D, D)
    o = o.transpose(0, 2, 1, 3).reshape(B, HH, WW, KD)
    y = (mxq(o, 3, "e4m3") @ unpack4(Wo_words, Wo_scales)) + f64(bo)
    return y.reshape(B, HH * WW, E)

@@ -1,0 +1,161 @@
+from contextlib import ExitStack
+
+import concourse.mybir as mybir
+from concourse.masks import make_identity
+
+BF16 = mybir.dt.bfloat16
+F32 = mybir.dt.float32
+I32 = mybir.dt.int32
+U8 = mybir.dt.uint8
+U32 = mybir.dt.uint32
+FP8X4 = mybir.dt.float8_e4m3fn_x4
+FP4X4 = mybir.dt.float4_e2m1fn_x4
+
+P = 128
+HEIGHT, WIDTH, HEADS, D = 512, 4, 8, 128
+KD = HEADS * D
+E_OUT = 1024
+PACK = 4
+K_PASS = P * PACK
+PASSES = KD // K_PASS
+PAIRS = PACK // 2
+N_TILE = 512
+N_HALVES = E_OUT // N_TILE
+H_TILES = HEIGHT // P
+ROW_TILES = H_TILES * WIDTH
+SCALE_ROWS = K_PASS // 32
+QUADRANTS = 4
+
+FLOPS = 2 * HEIGHT * WIDTH * KD * E_OUT + 2 * HEIGHT * WIDTH * HEADS * D * D
+
+
+def tile_linear_retention_pb_kernel(tc, ret_w, kv_h, Wo_words, Wo_scales, bo, out):
+    nc = tc.nc
+    out_rows = out[0].rearrange("(h w) n -> h w n", w=WIDTH)
+
+    with ExitStack() as ctx:
+        ctx.enter_context(tc.manual_schedule())
+        keep = ctx.enter_context(tc.tile_pool(name="keep", bufs=1))
+        stream = ctx.enter_context(tc.tile_pool(name="stream", bufs=3))
+        results = ctx.enter_context(tc.tile_pool(name="results", bufs=6))
+        psum = ctx.enter_context(tc.psum_pool(name="psum", bufs=1))
+
+        w_words = keep.tile([P, PASSES, 2 * E_OUT], U8, align_bytes=64)
+        w_scales = keep.tile([P, PASSES, E_OUT], U8, align_bytes=64)
+        bias_row = keep.tile([P, E_OUT], BF16)
+        ones = keep.tile([P, P], BF16)
+        bias = keep.tile([P, E_OUT], F32)
+        ident_bf16 = keep.tile([P, P], BF16)
+        ident_f32 = keep.tile([P, P], F32)
+
+        nc.vector.memset(w_scales[:].bitcast(I32), 0)
+        nc.vector.memset(bias_row[:], 0.0)
+        nc.vector.memset(ones[:], 1.0)
+        make_identity(nc, ident_bf16[:])
+        make_identity(nc, ident_f32[:])
+        nc.scalar.dma_start(out=bias_row[0:1, :], in_=bo.unsqueeze(0))
+
+        ret_sb = {}
+        kv_sb = {}
+
+        def load_ret(r):
+            ht, w = divmod(r, WIDTH)
+            ret_sb[r] = keep.tile([P, HEADS, D], BF16, name="ret%d" % r)
+            nc.sync.dma_start(out=ret_sb[r][:], in_=ret_w[0, ht * P : (ht + 1) * P, w])
+
+        for w in range(WIDTH):
+            load_ret(w)
+            kv_sb[w] = keep.tile([P, HEADS, D], BF16, name="kv%d" % w)
+            nc.sync.dma_start(out=kv_sb[w][:], in_=kv_h[0, w].rearrange("n e f -> e n f"))
+        for quadrant in range(QUADRANTS):
+            nc.sync.dma_start(
+                out=w_scales[32 * quadrant : 32 * quadrant + 4].bitcast(I32),
+                in_=Wo_scales.bitcast(I32)[:, 4 * quadrant : 4 * quadrant + 4, :].rearrange("g q n -> q g n"),
+            )
+        nc.sync.dma_start(out=w_words[:].bitcast(I32), in_=Wo_words.bitcast(I32).rearrange("g p b -> p g b"))
+        for r in range(WIDTH, ROW_TILES):
+            load_ret(r)
+
+        def broadcast_bias():
+            for half in range(N_HALVES):
+                cols = slice(half * N_TILE, (half + 1) * N_TILE)
+                bias_ps = psum.tile([P, N_TILE], F32, tag="y_ps", bufs=4)
+                nc.tensor.matmul(bias_ps[:], lhsT=ones[:], rhs=bias_row[:, cols], start=True, stop=True)
+                nc.vector.tensor_copy(out=bias[:, cols], in_=bias_ps[:])
+
+        ret_t = {}
+        o_words = {}
+        grouped = {}
+        codes = {}
+        scales = {}
+
+        def transpose_ret(r):
+            ret_t_ps = psum.tile([P, HEADS, P], BF16, tag="ret_t_ps", bufs=2)
+            for n in range(HEADS):
+                nc.tensor.transpose(ret_t_ps[:, n, :], ret_sb[r][:, n, :], ident_bf16[:])
+            ret_t[r] = stream.tile([P, HEADS, P], BF16, name="ret_t")
+            nc.scalar.copy(out=ret_t[r][:], in_=ret_t_ps[:])
+
+        def read_out(r):
+            w = r % WIDTH
+            o_ps = psum.tile([P, KD], BF16, tag="o_ps")
+            for n in range(HEADS):
+                nc.tensor.matmul(
+                    o_ps[:, n * D : (n + 1) * D], lhsT=ret_t[r][:, n, :], rhs=kv_sb[w][:, n, :], start=True, stop=True
+                )
+            o_words[r] = stream.tile([P, PASSES, PAIRS, P], F32, name="o_words")
+            nc.scalar.copy(
+                out=o_words[r][:],
+                in_=o_ps[:].bitcast(F32).rearrange("row (g p u) -> row g u p", g=PASSES, u=PAIRS),
+            )
+
+        def transpose_o(r):
+            o_t_ps = psum.tile([P, PASSES, PAIRS, P], F32, tag="o_t_ps")
+            for g in range(PASSES):
+                for u in range(PAIRS):
+                    nc.tensor.transpose(o_t_ps[:, g, u, :], o_words[r][:, g, u, :], ident_f32[:])
+            grouped[r] = stream.tile([P, PASSES * P * PACK], BF16, name="grouped", align_bytes=64)
+            nc.vector.tensor_copy(
+                out=grouped[r][:].bitcast(F32).rearrange("p (g row u) -> p g row u", g=PASSES, u=PAIRS),
+                in_=o_t_ps[:].rearrange("p g u row -> p g row u"),
+            )
+
+        def quantise(r):
+            codes[r] = stream.tile([P, PASSES * P], U32, name="codes", align_bytes=64)
+            scales[r] = stream.tile([P, PASSES * P], U8, name="scales", align_bytes=64)
+            nc.vector.quantize_mx(out=codes[r][:].bitcast(FP8X4), scales=scales[r][:], in_=grouped[r][:])
+
+        def project(r, half):
+            ht, w = divmod(r, WIDTH)
+            cols = slice(half * N_TILE, (half + 1) * N_TILE)
+            y_ps = psum.tile([P, N_TILE], F32, tag="y_ps", bufs=4)
+            for g in range(PASSES):
+                rows = slice(g * P, (g + 1) * P)
+                nc.tensor.matmul_mx(
+                    out=y_ps[:],
+                    lhsT=codes[r][:, rows].bitcast(FP8X4),
+                    lhsT_scale=scales[r][:, rows],
+                    rhs=w_words[:, g, 2 * half * N_TILE : 2 * (half + 1) * N_TILE].bitcast(FP4X4),
+                    rhs_scale=w_scales[:, g, cols],
+                    start=(g == 0),
+                    stop=(g == PASSES - 1),
+                )
+            y = results.tile([P, N_TILE], F32)
+            nc.vector.tensor_tensor(out=y[:], in0=y_ps[:], in1=bias[:, cols], op=mybir.AluOpType.add)
+            nc.sync.dma_start(out=out_rows[ht * P : (ht + 1) * P, w, cols], in_=y[:])
+
+        for step in range(ROW_TILES + 3):
+            if 0 <= step - 1 < ROW_TILES:
+                read_out(step - 1)
+            if step < ROW_TILES:
+                transpose_ret(step)
+            if step == 0:
+                broadcast_bias()
+            if 0 <= step - 2 < ROW_TILES:
+                transpose_o(step - 2)
+            if 0 <= step - 3 < ROW_TILES:
+                project(step - 3, 0)
+            if 0 <= step - 2 < ROW_TILES:
+                quantise(step - 2)
+            if 0 <= step - 3 < ROW_TILES:
+                project(step - 3, 1)

@@ -23,7 +23,7 @@ N_TILE = 512
 N_HALVES = E_OUT // N_TILE
 H_TILES = HEIGHT // P
 ROW_TILES = H_TILES * WIDTH
-SCALE_ROWS = K_PASS // 32
+LAG_READ_OUT, LAG_TRANSPOSE_O, LAG_PROJECT = 2, 3, 4
 QUADRANTS = 4
 
 FLOPS = 2 * HEIGHT * WIDTH * KD * E_OUT + 2 * HEIGHT * WIDTH * HEADS * D * D
@@ -36,7 +36,7 @@ def tile_linear_retention_pb_kernel(tc, ret_w, kv_h, Wo_words, Wo_scales, bo, ou
     with ExitStack() as ctx:
         ctx.enter_context(tc.manual_schedule())
         keep = ctx.enter_context(tc.tile_pool(name="keep", bufs=1))
-        stream = ctx.enter_context(tc.tile_pool(name="stream", bufs=3))
+        stream = ctx.enter_context(tc.tile_pool(name="stream", bufs=4))
         results = ctx.enter_context(tc.tile_pool(name="results", bufs=6))
         psum = ctx.enter_context(tc.psum_pool(name="psum", bufs=1))
 
@@ -48,8 +48,8 @@ def tile_linear_retention_pb_kernel(tc, ret_w, kv_h, Wo_words, Wo_scales, bo, ou
         ident_bf16 = keep.tile([P, P], BF16)
         ident_f32 = keep.tile([P, P], F32)
 
-        nc.vector.memset(w_scales[:].bitcast(I32), 0)
         nc.vector.memset(bias_row[:], 0.0)
+        nc.vector.memset(w_scales[:].bitcast(I32), 0)
         nc.vector.memset(ones[:], 1.0)
         make_identity(nc, ident_bf16[:])
         make_identity(nc, ident_f32[:])
@@ -58,23 +58,24 @@ def tile_linear_retention_pb_kernel(tc, ret_w, kv_h, Wo_words, Wo_scales, bo, ou
         ret_sb = {}
         kv_sb = {}
 
-        def load_ret(r):
-            ht, w = divmod(r, WIDTH)
-            ret_sb[r] = keep.tile([P, HEADS, D], BF16, name="ret%d" % r)
-            nc.sync.dma_start(out=ret_sb[r][:], in_=ret_w[0, ht * P : (ht + 1) * P, w])
+        def load_weight():
+            for quadrant in range(QUADRANTS):
+                nc.sync.dma_start(
+                    out=w_scales[32 * quadrant : 32 * quadrant + 4].bitcast(I32),
+                    in_=Wo_scales.bitcast(I32)[:, 4 * quadrant : 4 * quadrant + 4, :].rearrange("g q n -> q g n"),
+                )
+            nc.sync.dma_start(out=w_words[:].bitcast(I32), in_=Wo_words.bitcast(I32).rearrange("g p b -> p g b"))
 
         for w in range(WIDTH):
-            load_ret(w)
-            kv_sb[w] = keep.tile([P, HEADS, D], BF16, name="kv%d" % w)
-            nc.sync.dma_start(out=kv_sb[w][:], in_=kv_h[0, w].rearrange("n e f -> e n f"))
-        for quadrant in range(QUADRANTS):
-            nc.sync.dma_start(
-                out=w_scales[32 * quadrant : 32 * quadrant + 4].bitcast(I32),
-                in_=Wo_scales.bitcast(I32)[:, 4 * quadrant : 4 * quadrant + 4, :].rearrange("g q n -> q g n"),
-            )
-        nc.sync.dma_start(out=w_words[:].bitcast(I32), in_=Wo_words.bitcast(I32).rearrange("g p b -> p g b"))
-        for r in range(WIDTH, ROW_TILES):
-            load_ret(r)
+            for ht in range(H_TILES):
+                r = w * H_TILES + ht
+                ret_sb[r] = keep.tile([P, HEADS, D], BF16, name="ret%d" % r)
+                nc.sync.dma_start(out=ret_sb[r][:], in_=ret_w[0, ht * P : (ht + 1) * P, w])
+                if ht == 0:
+                    kv_sb[w] = keep.tile([P, HEADS, D], BF16, name="kv%d" % w)
+                    nc.sync.dma_start(out=kv_sb[w][:], in_=kv_h[0, w].rearrange("n e f -> e n f"))
+            if w == 0:
+                load_weight()
 
         def broadcast_bias():
             for half in range(N_HALVES):
@@ -97,7 +98,7 @@ def tile_linear_retention_pb_kernel(tc, ret_w, kv_h, Wo_words, Wo_scales, bo, ou
             nc.scalar.copy(out=ret_t[r][:], in_=ret_t_ps[:])
 
         def read_out(r):
-            w = r % WIDTH
+            w = r // H_TILES
             o_ps = psum.tile([P, KD], BF16, tag="o_ps")
             for n in range(HEADS):
                 nc.tensor.matmul(
@@ -115,7 +116,7 @@ def tile_linear_retention_pb_kernel(tc, ret_w, kv_h, Wo_words, Wo_scales, bo, ou
                 for u in range(PAIRS):
                     nc.tensor.transpose(o_t_ps[:, g, u, :], o_words[r][:, g, u, :], ident_f32[:])
             grouped[r] = stream.tile([P, PASSES * P * PACK], BF16, name="grouped", align_bytes=64)
-            nc.vector.tensor_copy(
+            nc.scalar.copy(
                 out=grouped[r][:].bitcast(F32).rearrange("p (g row u) -> p g row u", g=PASSES, u=PAIRS),
                 in_=o_t_ps[:].rearrange("p g u row -> p g row u"),
             )
@@ -126,7 +127,7 @@ def tile_linear_retention_pb_kernel(tc, ret_w, kv_h, Wo_words, Wo_scales, bo, ou
             nc.vector.quantize_mx(out=codes[r][:].bitcast(FP8X4), scales=scales[r][:], in_=grouped[r][:])
 
         def project(r, half):
-            ht, w = divmod(r, WIDTH)
+            w, ht = divmod(r, H_TILES)
             cols = slice(half * N_TILE, (half + 1) * N_TILE)
             y_ps = psum.tile([P, N_TILE], F32, tag="y_ps", bufs=4)
             for g in range(PASSES):
@@ -144,18 +145,16 @@ def tile_linear_retention_pb_kernel(tc, ret_w, kv_h, Wo_words, Wo_scales, bo, ou
             nc.vector.tensor_tensor(out=y[:], in0=y_ps[:], in1=bias[:, cols], op=mybir.AluOpType.add)
             nc.sync.dma_start(out=out_rows[ht * P : (ht + 1) * P, w, cols], in_=y[:])
 
-        for step in range(ROW_TILES + 3):
-            if 0 <= step - 1 < ROW_TILES:
-                read_out(step - 1)
+        for step in range(ROW_TILES + LAG_PROJECT):
+            if 0 <= step - LAG_READ_OUT < ROW_TILES:
+                read_out(step - LAG_READ_OUT)
             if step < ROW_TILES:
                 transpose_ret(step)
-            if step == 0:
+            if 0 <= step - LAG_TRANSPOSE_O < ROW_TILES:
+                transpose_o(step - LAG_TRANSPOSE_O)
+                quantise(step - LAG_TRANSPOSE_O)
+            if step == LAG_PROJECT - 1:
                 broadcast_bias()
-            if 0 <= step - 2 < ROW_TILES:
-                transpose_o(step - 2)
-            if 0 <= step - 3 < ROW_TILES:
-                project(step - 3, 0)
-            if 0 <= step - 2 < ROW_TILES:
-                quantise(step - 2)
-            if 0 <= step - 3 < ROW_TILES:
-                project(step - 3, 1)
+            if 0 <= step - LAG_PROJECT < ROW_TILES:
+                for half in range(N_HALVES):
+                    project(step - LAG_PROJECT, half)

@@ -18,6 +18,7 @@ E_OUT = 1024
 PACK = 4
 K_PASS = P * PACK
 PASSES = KD // K_PASS
+HEADS_PER_PASS = K_PASS // D
 PAIRS = PACK // 2
 N_TILE = 512
 N_HALVES = E_OUT // N_TILE
@@ -71,7 +72,7 @@ def tile_linear_retention_pb_kernel(tc, ret_w, kv_h, Wo_words, Wo_scales, bo, ou
                 r = w * H_TILES + ht
                 ret_sb[r] = keep.tile([P, HEADS, D], BF16, name="ret%d" % r)
                 nc.sync.dma_start(out=ret_sb[r][:], in_=ret_w[0, ht * P : (ht + 1) * P, w])
-                if ht == 0:
+                if ht == 1:
                     kv_sb[w] = keep.tile([P, HEADS, D], BF16, name="kv%d" % w)
                     nc.sync.dma_start(out=kv_sb[w][:], in_=kv_h[0, w].rearrange("n e f -> e n f"))
             if w == 0:
@@ -85,6 +86,7 @@ def tile_linear_retention_pb_kernel(tc, ret_w, kv_h, Wo_words, Wo_scales, bo, ou
                 nc.vector.tensor_copy(out=bias[:, cols], in_=bias_ps[:])
 
         ret_t = {}
+        o_ps = {}
         o_words = {}
         grouped = {}
         codes = {}
@@ -97,17 +99,23 @@ def tile_linear_retention_pb_kernel(tc, ret_w, kv_h, Wo_words, Wo_scales, bo, ou
             ret_t[r] = stream.tile([P, HEADS, P], BF16, name="ret_t")
             nc.scalar.copy(out=ret_t[r][:], in_=ret_t_ps[:])
 
-        def read_out(r):
+        def read_out(r, g):
             w = r // H_TILES
-            o_ps = psum.tile([P, KD], BF16, tag="o_ps")
-            for n in range(HEADS):
+            if g == 0:
+                o_ps[r] = psum.tile([P, PASSES, K_PASS], BF16, name="o_ps")
+                o_words[r] = stream.tile([P, PASSES, PAIRS, P], F32, name="o_words")
+            for j in range(HEADS_PER_PASS):
+                n = g * HEADS_PER_PASS + j
                 nc.tensor.matmul(
-                    o_ps[:, n * D : (n + 1) * D], lhsT=ret_t[r][:, n, :], rhs=kv_sb[w][:, n, :], start=True, stop=True
+                    o_ps[r][:, g, j * D : (j + 1) * D],
+                    lhsT=ret_t[r][:, n, :],
+                    rhs=kv_sb[w][:, n, :],
+                    start=True,
+                    stop=True,
                 )
-            o_words[r] = stream.tile([P, PASSES, PAIRS, P], F32, name="o_words")
             nc.scalar.copy(
-                out=o_words[r][:],
-                in_=o_ps[:].bitcast(F32).rearrange("row (g p u) -> row g u p", g=PASSES, u=PAIRS),
+                out=o_words[r][:, g],
+                in_=o_ps[r][:, g, :].bitcast(F32).rearrange("row (p u) -> row u p", u=PAIRS),
             )
 
         def transpose_o(r):
@@ -147,12 +155,14 @@ def tile_linear_retention_pb_kernel(tc, ret_w, kv_h, Wo_words, Wo_scales, bo, ou
 
         for step in range(ROW_TILES + LAG_PROJECT):
             if 0 <= step - LAG_READ_OUT < ROW_TILES:
-                read_out(step - LAG_READ_OUT)
+                read_out(step - LAG_READ_OUT, 0)
             if step < ROW_TILES:
                 transpose_ret(step)
             if 0 <= step - LAG_TRANSPOSE_O < ROW_TILES:
                 transpose_o(step - LAG_TRANSPOSE_O)
                 quantise(step - LAG_TRANSPOSE_O)
+            if 0 <= step - LAG_READ_OUT < ROW_TILES:
+                read_out(step - LAG_READ_OUT, 1)
             if step == LAG_PROJECT - 1:
                 broadcast_bias()
             if 0 <= step - LAG_PROJECT < ROW_TILES:

@@ -25,6 +25,7 @@ N_HALVES = E_OUT // N_TILE
 H_TILES = HEIGHT // P
 ROW_TILES = H_TILES * WIDTH
 LAG_READ_OUT, LAG_TRANSPOSE_O, LAG_PROJECT = 2, 3, 4
+WARM_UP = 4
 QUADRANTS = 4
 
 FLOPS = 2 * HEIGHT * WIDTH * KD * E_OUT + 2 * HEIGHT * WIDTH * HEADS * D * D
@@ -43,18 +44,24 @@ def tile_linear_retention_pb_kernel(tc, ret_w, kv_h, Wo_words, Wo_scales, bo, ou
 
         w_words = keep.tile([P, PASSES, 2 * E_OUT], U8, align_bytes=64)
         w_scales = keep.tile([P, PASSES, E_OUT], U8, align_bytes=64)
+        bo_sb = keep.tile([1, E_OUT], BF16)
         bias_row = keep.tile([P, E_OUT], BF16)
-        ones = keep.tile([P, P], BF16)
+        ones = keep.tile([P, N_TILE], BF16)
         bias = keep.tile([P, E_OUT], F32)
         ident_bf16 = keep.tile([P, P], BF16)
         ident_f32 = keep.tile([P, P], F32)
 
-        nc.vector.memset(bias_row[:], 0.0)
-        nc.vector.memset(w_scales[:].bitcast(I32), 0)
+        nc.scalar.dma_start(out=bo_sb[:], in_=bo.unsqueeze(0))
         nc.vector.memset(ones[:], 1.0)
+        nc.vector.memset(w_scales[:].bitcast(I32), 0)
+        nc.vector.memset(bias_row[:], 0.0)
+        nc.vector.tensor_copy(out=bias_row[0:1, :], in_=bo_sb[:])
         make_identity(nc, ident_bf16[:])
         make_identity(nc, ident_f32[:])
-        nc.scalar.dma_start(out=bias_row[0:1, :], in_=bo.unsqueeze(0))
+
+        for i in range(WARM_UP):
+            warm_ps = psum.tile([P, N_TILE], F32, tag="y_ps", bufs=3)
+            nc.tensor.matmul(warm_ps[:], lhsT=ones[:, 0:P], rhs=ones[:], start=True, stop=True)
 
         ret_sb = {}
         kv_sb = {}
@@ -81,8 +88,8 @@ def tile_linear_retention_pb_kernel(tc, ret_w, kv_h, Wo_words, Wo_scales, bo, ou
         def broadcast_bias():
             for half in range(N_HALVES):
                 cols = slice(half * N_TILE, (half + 1) * N_TILE)
-                bias_ps = psum.tile([P, N_TILE], F32, tag="y_ps", bufs=4)
-                nc.tensor.matmul(bias_ps[:], lhsT=ones[:], rhs=bias_row[:, cols], start=True, stop=True)
+                bias_ps = psum.tile([P, N_TILE], F32, tag="y_ps", bufs=3)
+                nc.tensor.matmul(bias_ps[:], lhsT=ones[:, 0:P], rhs=bias_row[:, cols], start=True, stop=True)
                 nc.vector.tensor_copy(out=bias[:, cols], in_=bias_ps[:])
 
         ret_t = {}
@@ -102,7 +109,7 @@ def tile_linear_retention_pb_kernel(tc, ret_w, kv_h, Wo_words, Wo_scales, bo, ou
         def read_out(r, g):
             w = r // H_TILES
             if g == 0:
-                o_ps[r] = psum.tile([P, PASSES, K_PASS], BF16, name="o_ps")
+                o_ps[r] = psum.tile([P, PASSES, K_PASS], BF16, name="o_ps", bufs=2)
                 o_words[r] = stream.tile([P, PASSES, PAIRS, P], F32, name="o_words")
             for j in range(HEADS_PER_PASS):
                 n = g * HEADS_PER_PASS + j
@@ -137,7 +144,7 @@ def tile_linear_retention_pb_kernel(tc, ret_w, kv_h, Wo_words, Wo_scales, bo, ou
         def project(r, half):
             w, ht = divmod(r, H_TILES)
             cols = slice(half * N_TILE, (half + 1) * N_TILE)
-            y_ps = psum.tile([P, N_TILE], F32, tag="y_ps", bufs=4)
+            y_ps = psum.tile([P, N_TILE], F32, tag="y_ps", bufs=3)
             for g in range(PASSES):
                 rows = slice(g * P, (g + 1) * P)
                 nc.tensor.matmul_mx(
@@ -158,13 +165,13 @@ def tile_linear_retention_pb_kernel(tc, ret_w, kv_h, Wo_words, Wo_scales, bo, ou
                 read_out(step - LAG_READ_OUT, 0)
             if step < ROW_TILES:
                 transpose_ret(step)
+            if step == LAG_READ_OUT - 1:
+                broadcast_bias()
             if 0 <= step - LAG_TRANSPOSE_O < ROW_TILES:
                 transpose_o(step - LAG_TRANSPOSE_O)
                 quantise(step - LAG_TRANSPOSE_O)
             if 0 <= step - LAG_READ_OUT < ROW_TILES:
                 read_out(step - LAG_READ_OUT, 1)
-            if step == LAG_PROJECT - 1:
-                broadcast_bias()
             if 0 <= step - LAG_PROJECT < ROW_TILES:
                 for half in range(N_HALVES):
                     project(step - LAG_PROJECT, half)

@@ -25,6 +25,10 @@ N_HALVES = E_OUT // N_TILE
 H_TILES = HEIGHT // P
 ROW_TILES = H_TILES * WIDTH
 LAG_READ_OUT, LAG_TRANSPOSE_O, LAG_PROJECT = 2, 3, 4
+PAIR = 2
+GROUPS = ROW_TILES // PAIR
+VECTOR_GROUPS = 3
+CHUNKS = 4
 WARM_UP = 4
 QUADRANTS = 4
 
@@ -48,7 +52,6 @@ def tile_linear_retention_pb_kernel(tc, ret_w, kv_h, Wo_words, Wo_scales, bo, ou
         bias_row = keep.tile([P, E_OUT], BF16)
         ones = keep.tile([P, N_TILE], BF16)
         bias = keep.tile([P, E_OUT], F32)
-        ident_bf16 = keep.tile([P, P], BF16)
         ident_f32 = keep.tile([P, P], F32)
 
         nc.scalar.dma_start(out=bo_sb[:], in_=bo.unsqueeze(0))
@@ -56,14 +59,12 @@ def tile_linear_retention_pb_kernel(tc, ret_w, kv_h, Wo_words, Wo_scales, bo, ou
         nc.vector.memset(w_scales[:].bitcast(I32), 0)
         nc.vector.memset(bias_row[:], 0.0)
         nc.vector.tensor_copy(out=bias_row[0:1, :], in_=bo_sb[:])
-        make_identity(nc, ident_bf16[:])
         make_identity(nc, ident_f32[:])
 
         for i in range(WARM_UP):
             warm_ps = psum.tile([P, N_TILE], F32, tag="y_ps", bufs=3)
             nc.tensor.matmul(warm_ps[:], lhsT=ones[:, 0:P], rhs=ones[:], start=True, stop=True)
 
-        ret_sb = {}
         kv_sb = {}
 
         def load_weight():
@@ -74,16 +75,51 @@ def tile_linear_retention_pb_kernel(tc, ret_w, kv_h, Wo_words, Wo_scales, bo, ou
                 )
             nc.sync.dma_start(out=w_words[:].bitcast(I32), in_=Wo_words.bitcast(I32).rearrange("g p b -> p g b"))
 
-        for w in range(WIDTH):
-            for ht in range(H_TILES):
-                r = w * H_TILES + ht
-                ret_sb[r] = keep.tile([P, HEADS, D], BF16, name="ret%d" % r)
-                nc.sync.dma_start(out=ret_sb[r][:], in_=ret_w[0, ht * P : (ht + 1) * P, w])
-                if ht == 1:
-                    kv_sb[w] = keep.tile([P, HEADS, D], BF16, name="kv%d" % w)
-                    nc.sync.dma_start(out=kv_sb[w][:], in_=kv_h[0, w].rearrange("n e f -> e n f"))
-            if w == 0:
-                load_weight()
+        ret_rows = {}
+        ret_pairs = {}
+
+        def load_group(d, pieces):
+            w, hd = divmod(d, H_TILES // PAIR)
+            ret_rows[d] = keep.tile([P, PAIR, KD], BF16, name="rows%d" % d)
+            ret_pairs[d] = keep.tile([P, KD, PAIR], BF16, name="pairs%d" % d)
+            rows = ret_w[0, hd * PAIR * P : (hd + 1) * PAIR * P, w].rearrange("(p s) n e -> p s (n e)", s=PAIR)
+            for c in range(pieces):
+                cols = slice(c * KD // pieces, (c + 1) * KD // pieces)
+                nc.sync.dma_start(out=ret_rows[d][:, :, cols], in_=rows[:, :, cols])
+
+        def load_state(w):
+            kv_sb[w] = keep.tile([P, HEADS, D], BF16, name="kv%d" % w)
+            nc.sync.dma_start(out=kv_sb[w][:], in_=kv_h[0, w].rearrange("n e f -> e n f"))
+
+        def interleave(d):
+            for c in range(CHUNKS):
+                cols = slice(c * KD // CHUNKS, (c + 1) * KD // CHUNKS)
+                by_column = ret_rows[d][:, :, cols].rearrange("p s c -> p c s")
+                if d < VECTOR_GROUPS:
+                    nc.vector.tensor_copy(out=ret_pairs[d][:, cols, :], in_=by_column)
+                else:
+                    nc.gpsimd.tensor_scalar(
+                        out=ret_pairs[d][:, cols, :],
+                        in0=by_column,
+                        scalar1=1.0,
+                        scalar2=0.0,
+                        op0=mybir.AluOpType.mult,
+                        op1=mybir.AluOpType.add,
+                    )
+
+        load_group(0, CHUNKS)
+        load_state(0)
+        load_group(1, 1)
+        load_group(2, 1)
+        load_weight()
+        load_state(1)
+        load_group(3, 1)
+        for d in range(4, GROUPS):
+            if d % 2 == 0:
+                load_state(d // 2)
+            load_group(d, 1)
+        for d in range(GROUPS):
+            interleave(d)
 
         def broadcast_bias():
             for half in range(N_HALVES):
@@ -99,12 +135,16 @@ def tile_linear_retention_pb_kernel(tc, ret_w, kv_h, Wo_words, Wo_scales, bo, ou
         codes = {}
         scales = {}
 
-        def transpose_ret(r):
-            ret_t_ps = psum.tile([P, HEADS, P], BF16, tag="ret_t_ps", bufs=2)
-            for n in range(HEADS):
-                nc.tensor.transpose(ret_t_ps[:, n, :], ret_sb[r][:, n, :], ident_bf16[:])
-            ret_t[r] = stream.tile([P, HEADS, P], BF16, name="ret_t")
-            nc.scalar.copy(out=ret_t[r][:], in_=ret_t_ps[:])
+        def transpose_ret(step):
+            d, b = divmod(step, PAIR)
+            if b == 0:
+                ret_t[d] = stream.tile([P, HEADS, P], F32, name="ret_t")
+            words = ret_pairs[d][:].rearrange("p c s -> p (c s)").bitcast(F32)
+            ret_t_ps = psum.tile([P, HEADS // PAIR, P], F32, tag="ret_t_ps", bufs=2)
+            for j in range(HEADS // PAIR):
+                n = b * (HEADS // PAIR) + j
+                nc.tensor.transpose(ret_t_ps[:, j, :], words[:, n * D : (n + 1) * D], ident_f32[:])
+            nc.scalar.copy(out=ret_t[d][:, b * (HEADS // PAIR) : (b + 1) * (HEADS // PAIR), :], in_=ret_t_ps[:])
 
         def read_out(r, g):
             w = r // H_TILES
@@ -115,7 +155,7 @@ def tile_linear_retention_pb_kernel(tc, ret_w, kv_h, Wo_words, Wo_scales, bo, ou
                 n = g * HEADS_PER_PASS + j
                 nc.tensor.matmul(
                     o_ps[r][:, g, j * D : (j + 1) * D],
-                    lhsT=ret_t[r][:, n, :],
+                    lhsT=ret_t[r // PAIR][:, n, :].bitcast(BF16)[:, (r % PAIR) * P : (r % PAIR + 1) * P],
                     rhs=kv_sb[w][:, n, :],
                     start=True,
                     stop=True,

@@ -24,11 +24,7 @@ N_TILE = 512
 N_HALVES = E_OUT // N_TILE
 H_TILES = HEIGHT // P
 ROW_TILES = H_TILES * WIDTH
-LAG_READ_OUT, LAG_TRANSPOSE_O, LAG_PROJECT = 2, 3, 4
-PAIR = 2
-GROUPS = ROW_TILES // PAIR
-VECTOR_GROUPS = 3
-CHUNKS = 4
+EARLY_TILES = 3
 WARM_UP = 4
 QUADRANTS = 4
 
@@ -52,6 +48,7 @@ def tile_linear_retention_pb_kernel(tc, ret_w, kv_h, Wo_words, Wo_scales, bo, ou
         bias_row = keep.tile([P, E_OUT], BF16)
         ones = keep.tile([P, N_TILE], BF16)
         bias = keep.tile([P, E_OUT], F32)
+        ident_bf16 = keep.tile([P, P], BF16)
         ident_f32 = keep.tile([P, P], F32)
 
         nc.scalar.dma_start(out=bo_sb[:], in_=bo.unsqueeze(0))
@@ -59,13 +56,29 @@ def tile_linear_retention_pb_kernel(tc, ret_w, kv_h, Wo_words, Wo_scales, bo, ou
         nc.vector.memset(w_scales[:].bitcast(I32), 0)
         nc.vector.memset(bias_row[:], 0.0)
         nc.vector.tensor_copy(out=bias_row[0:1, :], in_=bo_sb[:])
+        make_identity(nc, ident_bf16[:])
         make_identity(nc, ident_f32[:])
 
-        for i in range(WARM_UP):
-            warm_ps = psum.tile([P, N_TILE], F32, tag="y_ps", bufs=3)
-            nc.tensor.matmul(warm_ps[:], lhsT=ones[:, 0:P], rhs=ones[:], start=True, stop=True)
+        def keep_warm(times):
+            for i in range(times):
+                warm_ps = psum.tile([P, N_TILE], F32, tag="y_ps", bufs=3)
+                nc.tensor.matmul(warm_ps[:], lhsT=ones[:, 0:P], rhs=ones[:], start=True, stop=True)
 
+        keep_warm(WARM_UP)
+
+        ret_rows = {}
         kv_sb = {}
+
+        def load_rows(r, heads=slice(0, HEADS)):
+            w, ht = divmod(r, H_TILES)
+            if r not in ret_rows:
+                ret_rows[r] = keep.tile([P, HEADS, D], BF16, name="rows%d" % r)
+            nc.sync.dma_start(out=ret_rows[r][:, heads, :], in_=ret_w[0, ht * P : (ht + 1) * P, w, heads])
+
+        def load_state(w, heads=slice(0, HEADS)):
+            if w not in kv_sb:
+                kv_sb[w] = keep.tile([P, HEADS, D], BF16, name="kv%d" % w)
+            nc.sync.dma_start(out=kv_sb[w][:, heads, :], in_=kv_h[0, w, heads].rearrange("n e f -> e n f"))
 
         def load_weight():
             for quadrant in range(QUADRANTS):
@@ -75,51 +88,17 @@ def tile_linear_retention_pb_kernel(tc, ret_w, kv_h, Wo_words, Wo_scales, bo, ou
                 )
             nc.sync.dma_start(out=w_words[:].bitcast(I32), in_=Wo_words.bitcast(I32).rearrange("g p b -> p g b"))
 
-        ret_rows = {}
-        ret_pairs = {}
-
-        def load_group(d, pieces):
-            w, hd = divmod(d, H_TILES // PAIR)
-            ret_rows[d] = keep.tile([P, PAIR, KD], BF16, name="rows%d" % d)
-            ret_pairs[d] = keep.tile([P, KD, PAIR], BF16, name="pairs%d" % d)
-            rows = ret_w[0, hd * PAIR * P : (hd + 1) * PAIR * P, w].rearrange("(p s) n e -> p s (n e)", s=PAIR)
-            for c in range(pieces):
-                cols = slice(c * KD // pieces, (c + 1) * KD // pieces)
-                nc.sync.dma_start(out=ret_rows[d][:, :, cols], in_=rows[:, :, cols])
-
-        def load_state(w):
-            kv_sb[w] = keep.tile([P, HEADS, D], BF16, name="kv%d" % w)
-            nc.sync.dma_start(out=kv_sb[w][:], in_=kv_h[0, w].rearrange("n e f -> e n f"))
-
-        def interleave(d):
-            for c in range(CHUNKS):
-                cols = slice(c * KD // CHUNKS, (c + 1) * KD // CHUNKS)
-                by_column = ret_rows[d][:, :, cols].rearrange("p s c -> p c s")
-                if d < VECTOR_GROUPS:
-                    nc.vector.tensor_copy(out=ret_pairs[d][:, cols, :], in_=by_column)
-                else:
-                    nc.gpsimd.tensor_scalar(
-                        out=ret_pairs[d][:, cols, :],
-                        in0=by_column,
-                        scalar1=1.0,
-                        scalar2=0.0,
-                        op0=mybir.AluOpType.mult,
-                        op1=mybir.AluOpType.add,
-                    )
-
-        load_group(0, CHUNKS)
-        load_state(0)
-        load_group(1, 1)
-        load_group(2, 1)
+        for g in range(PASSES):
+            heads = slice(g * HEADS_PER_PASS, (g + 1) * HEADS_PER_PASS)
+            load_rows(0, heads)
+            load_state(0, heads)
+        for r in range(1, H_TILES):
+            load_rows(r)
         load_weight()
-        load_state(1)
-        load_group(3, 1)
-        for d in range(4, GROUPS):
-            if d % 2 == 0:
-                load_state(d // 2)
-            load_group(d, 1)
-        for d in range(GROUPS):
-            interleave(d)
+        for r in range(H_TILES, ROW_TILES):
+            load_rows(r)
+            if r % H_TILES == 0:
+                load_state(r // H_TILES)
 
         def broadcast_bias():
             for half in range(N_HALVES):
@@ -135,35 +114,43 @@ def tile_linear_retention_pb_kernel(tc, ret_w, kv_h, Wo_words, Wo_scales, bo, ou
         codes = {}
         scales = {}
 
-        def transpose_ret(step):
-            d, b = divmod(step, PAIR)
-            if b == 0:
-                ret_t[d] = stream.tile([P, HEADS, P], F32, name="ret_t")
-            words = ret_pairs[d][:].rearrange("p c s -> p (c s)").bitcast(F32)
-            ret_t_ps = psum.tile([P, HEADS // PAIR, P], F32, tag="ret_t_ps", bufs=2)
-            for j in range(HEADS // PAIR):
-                n = b * (HEADS // PAIR) + j
-                nc.tensor.transpose(ret_t_ps[:, j, :], words[:, n * D : (n + 1) * D], ident_f32[:])
-            nc.scalar.copy(out=ret_t[d][:, b * (HEADS // PAIR) : (b + 1) * (HEADS // PAIR), :], in_=ret_t_ps[:])
+        def transpose_ret(r, heads=range(HEADS)):
+            if r not in ret_t:
+                ret_t[r] = stream.tile([P, HEADS, P], BF16, name="ret_t")
+            ret_t_ps = psum.tile([P, len(heads), P], BF16, tag="ret_t_ps", bufs=2)
+            for j, n in enumerate(heads):
+                nc.tensor.transpose(ret_t_ps[:, j, :], ret_rows[r][:, n, :], ident_bf16[:])
+            done = ret_t[r][:, heads[0] : heads[-1] + 1, :]
+            if r < EARLY_TILES:
+                nc.vector.tensor_copy(out=done, in_=ret_t_ps[:])
+            else:
+                nc.scalar.copy(out=done, in_=ret_t_ps[:])
 
-        def read_out(r, g):
+        def multiply(r, g):
             w = r // H_TILES
             if g == 0:
                 o_ps[r] = psum.tile([P, PASSES, K_PASS], BF16, name="o_ps", bufs=2)
-                o_words[r] = stream.tile([P, PASSES, PAIRS, P], F32, name="o_words")
             for j in range(HEADS_PER_PASS):
                 n = g * HEADS_PER_PASS + j
                 nc.tensor.matmul(
                     o_ps[r][:, g, j * D : (j + 1) * D],
-                    lhsT=ret_t[r // PAIR][:, n, :].bitcast(BF16)[:, (r % PAIR) * P : (r % PAIR + 1) * P],
+                    lhsT=ret_t[r][:, n, :],
                     rhs=kv_sb[w][:, n, :],
                     start=True,
                     stop=True,
                 )
+
+        def sort_words(r, g):
+            if g == 0:
+                o_words[r] = stream.tile([P, PASSES, PAIRS, P], F32, name="o_words")
             nc.scalar.copy(
                 out=o_words[r][:, g],
                 in_=o_ps[r][:, g, :].bitcast(F32).rearrange("row (p u) -> row u p", u=PAIRS),
             )
+
+        def read_out(r, g):
+            multiply(r, g)
+            sort_words(r, g)
 
         def transpose_o(r):
             o_t_ps = psum.tile([P, PASSES, PAIRS, P], F32, tag="o_t_ps")
@@ -181,37 +168,56 @@ def tile_linear_retention_pb_kernel(tc, ret_w, kv_h, Wo_words, Wo_scales, bo, ou
             scales[r] = stream.tile([P, PASSES * P], U8, name="scales", align_bytes=64)
             nc.vector.quantize_mx(out=codes[r][:].bitcast(FP8X4), scales=scales[r][:], in_=grouped[r][:])
 
-        def project(r, half):
+        def project(r):
             w, ht = divmod(r, H_TILES)
-            cols = slice(half * N_TILE, (half + 1) * N_TILE)
-            y_ps = psum.tile([P, N_TILE], F32, tag="y_ps", bufs=3)
-            for g in range(PASSES):
-                rows = slice(g * P, (g + 1) * P)
-                nc.tensor.matmul_mx(
-                    out=y_ps[:],
-                    lhsT=codes[r][:, rows].bitcast(FP8X4),
-                    lhsT_scale=scales[r][:, rows],
-                    rhs=w_words[:, g, 2 * half * N_TILE : 2 * (half + 1) * N_TILE].bitcast(FP4X4),
-                    rhs_scale=w_scales[:, g, cols],
-                    start=(g == 0),
-                    stop=(g == PASSES - 1),
-                )
-            y = results.tile([P, N_TILE], F32)
-            nc.vector.tensor_tensor(out=y[:], in0=y_ps[:], in1=bias[:, cols], op=mybir.AluOpType.add)
-            nc.sync.dma_start(out=out_rows[ht * P : (ht + 1) * P, w, cols], in_=y[:])
+            for half in range(N_HALVES):
+                cols = slice(half * N_TILE, (half + 1) * N_TILE)
+                y_ps = psum.tile([P, N_TILE], F32, tag="y_ps", bufs=3)
+                for g in range(PASSES):
+                    rows = slice(g * P, (g + 1) * P)
+                    nc.tensor.matmul_mx(
+                        out=y_ps[:],
+                        lhsT=codes[r][:, rows].bitcast(FP8X4),
+                        lhsT_scale=scales[r][:, rows],
+                        rhs=w_words[:, g, 2 * half * N_TILE : 2 * (half + 1) * N_TILE].bitcast(FP4X4),
+                        rhs_scale=w_scales[:, g, cols],
+                        start=(g == 0),
+                        stop=(g == PASSES - 1),
+                    )
+                y = results.tile([P, N_TILE], F32)
+                nc.vector.tensor_tensor(out=y[:], in0=y_ps[:], in1=bias[:, cols], op=mybir.AluOpType.add)
+                nc.sync.dma_start(out=out_rows[ht * P : (ht + 1) * P, w, cols], in_=y[:])
 
-        for step in range(ROW_TILES + LAG_PROJECT):
-            if 0 <= step - LAG_READ_OUT < ROW_TILES:
-                read_out(step - LAG_READ_OUT, 0)
-            if step < ROW_TILES:
-                transpose_ret(step)
-            if step == LAG_READ_OUT - 1:
-                broadcast_bias()
-            if 0 <= step - LAG_TRANSPOSE_O < ROW_TILES:
-                transpose_o(step - LAG_TRANSPOSE_O)
-                quantise(step - LAG_TRANSPOSE_O)
-            if 0 <= step - LAG_READ_OUT < ROW_TILES:
-                read_out(step - LAG_READ_OUT, 1)
-            if 0 <= step - LAG_PROJECT < ROW_TILES:
-                for half in range(N_HALVES):
-                    project(step - LAG_PROJECT, half)
+        for g in range(PASSES):
+            transpose_ret(0, range(g * HEADS_PER_PASS, (g + 1) * HEADS_PER_PASS))
+        read_out(0, 0)
+        broadcast_bias()
+        read_out(0, 1)
+        transpose_ret(1)
+        transpose_o(0)
+        quantise(0)
+        keep_warm(1)
+        transpose_ret(2)
+        for g in range(PASSES):
+            multiply(1, g)
+        for g in range(PASSES):
+            sort_words(1, g)
+        keep_warm(1)
+        transpose_ret(3)
+        read_out(2, 0)
+        transpose_o(1)
+        quantise(1)
+        read_out(2, 1)
+        project(0)
+
+        for r in range(3, ROW_TILES + 2):
+            if r < ROW_TILES:
+                read_out(r, 0)
+            if r + 1 < ROW_TILES:
+                transpose_ret(r + 1)
+            if r - 1 < ROW_TILES:
+                transpose_o(r - 1)
+                quantise(r - 1)
+            if r < ROW_TILES:
+                read_out(r, 1)
+            project(r - 2)

@@ -24,6 +24,9 @@ N_TILE = 512
 N_HALVES = E_OUT // N_TILE
 H_TILES = HEIGHT // P
 ROW_TILES = H_TILES * WIDTH
+PAIR = 2
+PLAIN_TILES = 4
+CHUNKS = 4
 EARLY_TILES = 3
 WARM_UP = 4
 QUADRANTS = 4
@@ -88,17 +91,41 @@ def tile_linear_retention_pb_kernel(tc, ret_w, kv_h, Wo_words, Wo_scales, bo, ou
                 )
             nc.sync.dma_start(out=w_words[:].bitcast(I32), in_=Wo_words.bitcast(I32).rearrange("g p b -> p g b"))
 
+        pair_rows = {}
+        ret_pairs = {}
+
+        def load_group(d):
+            w, hd = divmod(d, H_TILES // PAIR)
+            pair_rows[d] = keep.tile([P, PAIR, KD], BF16, name="pair_rows%d" % d)
+            rows = ret_w[0, hd * PAIR * P : (hd + 1) * PAIR * P, w].rearrange("(p s) n e -> p s (n e)", s=PAIR)
+            nc.sync.dma_start(out=pair_rows[d][:], in_=rows)
+
+        def interleave(d):
+            ret_pairs[d] = keep.tile([P, KD, PAIR], BF16, name="pairs%d" % d)
+            for c in range(CHUNKS):
+                cols = slice(c * KD // CHUNKS, (c + 1) * KD // CHUNKS)
+                nc.gpsimd.tensor_scalar(
+                    out=ret_pairs[d][:, cols, :],
+                    in0=pair_rows[d][:, :, cols].rearrange("p s c -> p c s"),
+                    scalar1=1.0,
+                    scalar2=0.0,
+                    op0=mybir.AluOpType.mult,
+                    op1=mybir.AluOpType.add,
+                )
+
         for g in range(PASSES):
             heads = slice(g * HEADS_PER_PASS, (g + 1) * HEADS_PER_PASS)
             load_rows(0, heads)
             load_state(0, heads)
         for r in range(1, H_TILES):
             load_rows(r)
-        load_weight()
-        for r in range(H_TILES, ROW_TILES):
-            load_rows(r)
-            if r % H_TILES == 0:
-                load_state(r // H_TILES)
+        for d in range(PLAIN_TILES // PAIR, ROW_TILES // PAIR):
+            load_group(d)
+            if d == 2:
+                load_weight()
+            if d * PAIR % H_TILES == 0:
+                load_state(d * PAIR // H_TILES)
+            interleave(d)
 
         def broadcast_bias():
             for half in range(N_HALVES):
@@ -126,15 +153,33 @@ def tile_linear_retention_pb_kernel(tc, ret_w, kv_h, Wo_words, Wo_scales, bo, ou
             else:
                 nc.scalar.copy(out=done, in_=ret_t_ps[:])
 
+        def transpose_pairs(step):
+            d, b = divmod(step, PAIR)
+            if b == 0:
+                ret_t[d * PAIR] = stream.tile([P, HEADS, P], F32, name="ret_t_pairs")
+            words = ret_pairs[d][:].rearrange("p c s -> p (c s)").bitcast(F32)
+            ret_t_ps = psum.tile([P, HEADS // PAIR, P], F32, tag="ret_t_ps", bufs=2)
+            heads = slice(b * (HEADS // PAIR), (b + 1) * (HEADS // PAIR))
+            for j in range(HEADS // PAIR):
+                n = b * (HEADS // PAIR) + j
+                nc.tensor.transpose(ret_t_ps[:, j, :], words[:, n * D : (n + 1) * D], ident_f32[:])
+            nc.scalar.copy(out=ret_t[d * PAIR][:, heads, :], in_=ret_t_ps[:])
+
+        def stationary(r, n):
+            if r < PLAIN_TILES:
+                return ret_t[r][:, n, :]
+            rows = slice((r % PAIR) * P, (r % PAIR + 1) * P)
+            return ret_t[r - r % PAIR][:, n, :].bitcast(BF16)[:, rows]
+
         def multiply(r, g):
             w = r // H_TILES
-            if g == 0:
-                o_ps[r] = psum.tile([P, PASSES, K_PASS], BF16, name="o_ps", bufs=2)
+            o_bank = psum.tile([P, K_PASS], BF16, tag="o_ps%d" % g)
+            o_ps[r, g] = o_bank
             for j in range(HEADS_PER_PASS):
                 n = g * HEADS_PER_PASS + j
                 nc.tensor.matmul(
-                    o_ps[r][:, g, j * D : (j + 1) * D],
-                    lhsT=ret_t[r][:, n, :],
+                    o_ps[r, g][:, j * D : (j + 1) * D],
+                    lhsT=stationary(r, n),
                     rhs=kv_sb[w][:, n, :],
                     start=True,
                     stop=True,
@@ -145,7 +190,7 @@ def tile_linear_retention_pb_kernel(tc, ret_w, kv_h, Wo_words, Wo_scales, bo, ou
                 o_words[r] = stream.tile([P, PASSES, PAIRS, P], F32, name="o_words")
             nc.scalar.copy(
                 out=o_words[r][:, g],
-                in_=o_ps[r][:, g, :].bitcast(F32).rearrange("row (p u) -> row u p", u=PAIRS),
+                in_=o_ps[r, g][:].bitcast(F32).rearrange("row (p u) -> row u p", u=PAIRS),
             )
 
         def read_out(r, g):
@@ -204,17 +249,12 @@ def tile_linear_retention_pb_kernel(tc, ret_w, kv_h, Wo_words, Wo_scales, bo, ou
             sort_words(1, g)
         keep_warm(1)
         transpose_ret(3)
-        read_out(2, 0)
-        transpose_o(1)
-        quantise(1)
-        read_out(2, 1)
-        project(0)
 
-        for r in range(3, ROW_TILES + 2):
+        for r in range(2, ROW_TILES + 2):
             if r < ROW_TILES:
                 read_out(r, 0)
-            if r + 1 < ROW_TILES:
-                transpose_ret(r + 1)
+            if r + 2 < ROW_TILES:
+                transpose_pairs(r + 2)
             if r - 1 < ROW_TILES:
                 transpose_o(r - 1)
                 quantise(r - 1)

@@ -26,7 +26,6 @@ H_TILES = HEIGHT // P
 ROW_TILES = H_TILES * WIDTH
 PAIR = 2
 PLAIN_TILES = 4
-CHUNKS = 4
 EARLY_TILES = 3
 WARM_UP = 4
 QUADRANTS = 4
@@ -100,18 +99,14 @@ def tile_linear_retention_pb_kernel(tc, ret_w, kv_h, Wo_words, Wo_scales, bo, ou
             rows = ret_w[0, hd * PAIR * P : (hd + 1) * PAIR * P, w].rearrange("(p s) n e -> p s (n e)", s=PAIR)
             nc.sync.dma_start(out=pair_rows[d][:], in_=rows)
 
-        def interleave(d):
-            ret_pairs[d] = keep.tile([P, KD, PAIR], BF16, name="pairs%d" % d)
-            for c in range(CHUNKS):
-                cols = slice(c * KD // CHUNKS, (c + 1) * KD // CHUNKS)
-                nc.gpsimd.tensor_scalar(
-                    out=ret_pairs[d][:, cols, :],
-                    in0=pair_rows[d][:, :, cols].rearrange("p s c -> p c s"),
-                    scalar1=1.0,
-                    scalar2=0.0,
-                    op0=mybir.AluOpType.mult,
-                    op1=mybir.AluOpType.add,
-                )
+        def interleave(step):
+            d, b = divmod(step, PAIR)
+            if b == 0:
+                ret_pairs[d] = keep.tile([P, KD, PAIR], BF16, name="pairs%d" % d)
+            cols = slice(b * KD // PAIR, (b + 1) * KD // PAIR)
+            nc.vector.tensor_copy(
+                out=ret_pairs[d][:, cols, :], in_=pair_rows[d][:, :, cols].rearrange("p s c -> p c s")
+            )
 
         for g in range(PASSES):
             heads = slice(g * HEADS_PER_PASS, (g + 1) * HEADS_PER_PASS)
@@ -125,7 +120,6 @@ def tile_linear_retention_pb_kernel(tc, ret_w, kv_h, Wo_words, Wo_scales, bo, ou
                 load_weight()
             if d * PAIR % H_TILES == 0:
                 load_state(d * PAIR // H_TILES)
-            interleave(d)
 
         def broadcast_bias():
             for half in range(N_HALVES):
@@ -250,7 +244,10 @@ def tile_linear_retention_pb_kernel(tc, ret_w, kv_h, Wo_words, Wo_scales, bo, ou
         keep_warm(1)
         transpose_ret(3)
 
+        interleave(PLAIN_TILES)
         for r in range(2, ROW_TILES + 2):
+            if r + 3 < ROW_TILES:
+                interleave(r + 3)
             if r < ROW_TILES:
                 read_out(r, 0)
             if r + 2 < ROW_TILES:

@@ -229,6 +229,8 @@ def tile_linear_retention_pb_kernel(tc, ret_w, kv_h, Wo_words, Wo_scales, bo, ou
 
         for g in range(PASSES):
             transpose_ret(0, range(g * HEADS_PER_PASS, (g + 1) * HEADS_PER_PASS))
+            if g == 0:
+                keep_warm(2)
         read_out(0, 0)
         broadcast_bias()
         read_out(0, 1)
@@ -241,7 +243,6 @@ def tile_linear_retention_pb_kernel(tc, ret_w, kv_h, Wo_words, Wo_scales, bo, ou
             multiply(1, g)
         for g in range(PASSES):
             sort_words(1, g)
-        keep_warm(1)
         transpose_ret(3)
 
         interleave(PLAIN_TILES)
@@ -250,11 +251,11 @@ def tile_linear_retention_pb_kernel(tc, ret_w, kv_h, Wo_words, Wo_scales, bo, ou
                 interleave(r + 3)
             if r < ROW_TILES:
                 read_out(r, 0)
-            if r + 2 < ROW_TILES:
-                transpose_pairs(r + 2)
             if r - 1 < ROW_TILES:
                 transpose_o(r - 1)
                 quantise(r - 1)
+            if r + 2 < ROW_TILES:
+                transpose_pairs(r + 2)
             if r < ROW_TILES:
                 read_out(r, 1)
             project(r - 2)

from contextlib import ExitStack

import concourse.mybir as mybir
from concourse.masks import make_identity

BF16 = mybir.dt.bfloat16
F32 = mybir.dt.float32
I32 = mybir.dt.int32
U8 = mybir.dt.uint8
U32 = mybir.dt.uint32
FP8X4 = mybir.dt.float8_e4m3fn_x4
FP4X4 = mybir.dt.float4_e2m1fn_x4

P = 128
HEIGHT, WIDTH, HEADS, D = 512, 4, 8, 128
KD = HEADS * D
E_OUT = 1024
PACK = 4
K_PASS = P * PACK
PASSES = KD // K_PASS
HEADS_PER_PASS = K_PASS // D
PAIRS = PACK // 2
N_TILE = 512
N_HALVES = E_OUT // N_TILE
H_TILES = HEIGHT // P
ROW_TILES = H_TILES * WIDTH
PAIR = 2
PLAIN_TILES = 4
EARLY_TILES = 3
WARM_UP = 4
QUADRANTS = 4

FLOPS = 2 * HEIGHT * WIDTH * KD * E_OUT + 2 * HEIGHT * WIDTH * HEADS * D * D


def tile_linear_retention_pb_kernel(tc, ret_w, kv_h, Wo_words, Wo_scales, bo, out):
    nc = tc.nc
    out_rows = out[0].rearrange("(h w) n -> h w n", w=WIDTH)

    with ExitStack() as ctx:
        ctx.enter_context(tc.manual_schedule())
        keep = ctx.enter_context(tc.tile_pool(name="keep", bufs=1))
        stream = ctx.enter_context(tc.tile_pool(name="stream", bufs=4))
        results = ctx.enter_context(tc.tile_pool(name="results", bufs=6))
        psum = ctx.enter_context(tc.psum_pool(name="psum", bufs=1))

        w_words = keep.tile([P, PASSES, 2 * E_OUT], U8, align_bytes=64)
        w_scales = keep.tile([P, PASSES, E_OUT], U8, align_bytes=64)
        bo_sb = keep.tile([1, E_OUT], BF16)
        bias_row = keep.tile([P, E_OUT], BF16)
        ones = keep.tile([P, N_TILE], BF16)
        bias = keep.tile([P, E_OUT], F32)
        ident_bf16 = keep.tile([P, P], BF16)
        ident_f32 = keep.tile([P, P], F32)

        nc.scalar.dma_start(out=bo_sb[:], in_=bo.unsqueeze(0))
        nc.vector.memset(ones[:], 1.0)
        nc.vector.memset(w_scales[:].bitcast(I32), 0)
        nc.vector.memset(bias_row[:], 0.0)
        nc.vector.tensor_copy(out=bias_row[0:1, :], in_=bo_sb[:])
        make_identity(nc, ident_bf16[:])
        make_identity(nc, ident_f32[:])

        def keep_warm(times):
            for i in range(times):
                warm_ps = psum.tile([P, N_TILE], F32, tag="y_ps", bufs=3)
                nc.tensor.matmul(warm_ps[:], lhsT=ones[:, 0:P], rhs=ones[:], start=True, stop=True)

        keep_warm(WARM_UP)

        ret_rows = {}
        kv_sb = {}

        def load_rows(r, heads=slice(0, HEADS)):
            w, ht = divmod(r, H_TILES)
            if r not in ret_rows:
                ret_rows[r] = keep.tile([P, HEADS, D], BF16, name="rows%d" % r)
            nc.sync.dma_start(out=ret_rows[r][:, heads, :], in_=ret_w[0, ht * P : (ht + 1) * P, w, heads])

        def load_state(w, heads=slice(0, HEADS)):
            if w not in kv_sb:
                kv_sb[w] = keep.tile([P, HEADS, D], BF16, name="kv%d" % w)
            nc.sync.dma_start(out=kv_sb[w][:, heads, :], in_=kv_h[0, w, heads].rearrange("n e f -> e n f"))

        def load_weight():
            for quadrant in range(QUADRANTS):
                nc.sync.dma_start(
                    out=w_scales[32 * quadrant : 32 * quadrant + 4].bitcast(I32),
                    in_=Wo_scales.bitcast(I32)[:, 4 * quadrant : 4 * quadrant + 4, :].rearrange("g q n -> q g n"),
                )
            nc.sync.dma_start(out=w_words[:].bitcast(I32), in_=Wo_words.bitcast(I32).rearrange("g p b -> p g b"))

        pair_rows = {}
        ret_pairs = {}

        def load_group(d):
            w, hd = divmod(d, H_TILES // PAIR)
            pair_rows[d] = keep.tile([P, PAIR, KD], BF16, name="pair_rows%d" % d)
            rows = ret_w[0, hd * PAIR * P : (hd + 1) * PAIR * P, w].rearrange("(p s) n e -> p s (n e)", s=PAIR)
            nc.sync.dma_start(out=pair_rows[d][:], in_=rows)

        def interleave(step):
            d, b = divmod(step, PAIR)
            if b == 0:
                ret_pairs[d] = keep.tile([P, KD, PAIR], BF16, name="pairs%d" % d)
            cols = slice(b * KD // PAIR, (b + 1) * KD // PAIR)
            nc.vector.tensor_copy(
                out=ret_pairs[d][:, cols, :], in_=pair_rows[d][:, :, cols].rearrange("p s c -> p c s")
            )

        for g in range(PASSES):
            heads = slice(g * HEADS_PER_PASS, (g + 1) * HEADS_PER_PASS)
            load_rows(0, heads)
            load_state(0, heads)
        for r in range(1, H_TILES):
            load_rows(r)
        for d in range(PLAIN_TILES // PAIR, ROW_TILES // PAIR):
            load_group(d)
            if d == 2:
                load_weight()
            if d * PAIR % H_TILES == 0:
                load_state(d * PAIR // H_TILES)

        def broadcast_bias():
            for half in range(N_HALVES):
                cols = slice(half * N_TILE, (half + 1) * N_TILE)
                bias_ps = psum.tile([P, N_TILE], F32, tag="y_ps", bufs=3)
                nc.tensor.matmul(bias_ps[:], lhsT=ones[:, 0:P], rhs=bias_row[:, cols], start=True, stop=True)
                nc.vector.tensor_copy(out=bias[:, cols], in_=bias_ps[:])

        ret_t = {}
        o_ps = {}
        o_words = {}
        grouped = {}
        codes = {}
        scales = {}

        def transpose_ret(r, heads=range(HEADS)):
            if r not in ret_t:
                ret_t[r] = stream.tile([P, HEADS, P], BF16, name="ret_t")
            ret_t_ps = psum.tile([P, len(heads), P], BF16, tag="ret_t_ps", bufs=2)
            for j, n in enumerate(heads):
                nc.tensor.transpose(ret_t_ps[:, j, :], ret_rows[r][:, n, :], ident_bf16[:])
            done = ret_t[r][:, heads[0] : heads[-1] + 1, :]
            if r < EARLY_TILES:
                nc.vector.tensor_copy(out=done, in_=ret_t_ps[:])
            else:
                nc.scalar.copy(out=done, in_=ret_t_ps[:])

        def transpose_pairs(step):
            d, b = divmod(step, PAIR)
            if b == 0:
                ret_t[d * PAIR] = stream.tile([P, HEADS, P], F32, name="ret_t_pairs")
            words = ret_pairs[d][:].rearrange("p c s -> p (c s)").bitcast(F32)
            ret_t_ps = psum.tile([P, HEADS // PAIR, P], F32, tag="ret_t_ps", bufs=2)
            heads = slice(b * (HEADS // PAIR), (b + 1) * (HEADS // PAIR))
            for j in range(HEADS // PAIR):
                n = b * (HEADS // PAIR) + j
                nc.tensor.transpose(ret_t_ps[:, j, :], words[:, n * D : (n + 1) * D], ident_f32[:])
            nc.scalar.copy(out=ret_t[d * PAIR][:, heads, :], in_=ret_t_ps[:])

        def stationary(r, n):
            if r < PLAIN_TILES:
                return ret_t[r][:, n, :]
            rows = slice((r % PAIR) * P, (r % PAIR + 1) * P)
            return ret_t[r - r % PAIR][:, n, :].bitcast(BF16)[:, rows]

        def multiply(r, g):
            w = r // H_TILES
            o_bank = psum.tile([P, K_PASS], BF16, tag="o_ps%d" % g)
            o_ps[r, g] = o_bank
            for j in range(HEADS_PER_PASS):
                n = g * HEADS_PER_PASS + j
                nc.tensor.matmul(
                    o_ps[r, g][:, j * D : (j + 1) * D],
                    lhsT=stationary(r, n),
                    rhs=kv_sb[w][:, n, :],
                    start=True,
                    stop=True,
                )

        def sort_words(r, g):
            if g == 0:
                o_words[r] = stream.tile([P, PASSES, PAIRS, P], F32, name="o_words")
            nc.scalar.copy(
                out=o_words[r][:, g],
                in_=o_ps[r, g][:].bitcast(F32).rearrange("row (p u) -> row u p", u=PAIRS),
            )

        def read_out(r, g):
            multiply(r, g)
            sort_words(r, g)

        def transpose_o(r):
            o_t_ps = psum.tile([P, PASSES, PAIRS, P], F32, tag="o_t_ps")
            for g in range(PASSES):
                for u in range(PAIRS):
                    nc.tensor.transpose(o_t_ps[:, g, u, :], o_words[r][:, g, u, :], ident_f32[:])
            grouped[r] = stream.tile([P, PASSES * P * PACK], BF16, name="grouped", align_bytes=64)
            nc.scalar.copy(
                out=grouped[r][:].bitcast(F32).rearrange("p (g row u) -> p g row u", g=PASSES, u=PAIRS),
                in_=o_t_ps[:].rearrange("p g u row -> p g row u"),
            )

        def quantise(r):
            codes[r] = stream.tile([P, PASSES * P], U32, name="codes", align_bytes=64)
            scales[r] = stream.tile([P, PASSES * P], U8, name="scales", align_bytes=64)
            nc.vector.quantize_mx(out=codes[r][:].bitcast(FP8X4), scales=scales[r][:], in_=grouped[r][:])

        def project(r):
            w, ht = divmod(r, H_TILES)
            for half in range(N_HALVES):
                cols = slice(half * N_TILE, (half + 1) * N_TILE)
                y_ps = psum.tile([P, N_TILE], F32, tag="y_ps", bufs=3)
                for g in range(PASSES):
                    rows = slice(g * P, (g + 1) * P)
                    nc.tensor.matmul_mx(
                        out=y_ps[:],
                        lhsT=codes[r][:, rows].bitcast(FP8X4),
                        lhsT_scale=scales[r][:, rows],
                        rhs=w_words[:, g, 2 * half * N_TILE : 2 * (half + 1) * N_TILE].bitcast(FP4X4),
                        rhs_scale=w_scales[:, g, cols],
                        start=(g == 0),
                        stop=(g == PASSES - 1),
                    )
                y = results.tile([P, N_TILE], F32)
                nc.vector.tensor_tensor(out=y[:], in0=y_ps[:], in1=bias[:, cols], op=mybir.AluOpType.add)
                nc.sync.dma_start(out=out_rows[ht * P : (ht + 1) * P, w, cols], in_=y[:])

        for g in range(PASSES):
            transpose_ret(0, range(g * HEADS_PER_PASS, (g + 1) * HEADS_PER_PASS))
            if g == 0:
                keep_warm(2)
        read_out(0, 0)
        broadcast_bias()
        read_out(0, 1)
        transpose_ret(1)
        transpose_o(0)
        quantise(0)
        keep_warm(1)
        transpose_ret(2)
        for g in range(PASSES):
            multiply(1, g)
        for g in range(PASSES):
            sort_words(1, g)
        transpose_ret(3)

        interleave(PLAIN_TILES)
        for r in range(2, ROW_TILES + 2):
            if r + 3 < ROW_TILES:
                interleave(r + 3)
            if r < ROW_TILES:
                read_out(r, 0)
            if r - 1 < ROW_TILES:
                transpose_o(r - 1)
                quantise(r - 1)
            if r + 2 < ROW_TILES:
                transpose_pairs(r + 2)
            if r < ROW_TILES:
                read_out(r, 1)
            project(r - 2)
